import numpy as np
import ml_dtypes


def mxq(x, axis, fmt="e4m3"):
    dtype, down = {"e4m3": (ml_dtypes.float8_e4m3fn, 7), "e5m2": (ml_dtypes.float8_e5m2, 14)}[fmt]
    v = np.moveaxis(np.asarray(x, np.float32).astype(ml_dtypes.bfloat16).astype(np.float64), axis, -1)
    blocks = v.reshape(v.shape[:-1] + (-1, 32))
    amax = np.abs(blocks).max(-1, keepdims=True)
    byte = np.maximum(np.where(amax > 0, np.frexp(amax)[1] - 1 + 127, 0) - down, 1)
    scale = np.exp2(byte - 127.0)
    codes = (blocks / scale).astype(np.float32).astype(dtype).astype(np.float64)
    return np.moveaxis((codes * scale).reshape(v.shape), -1, axis)


WIDE = False


def mx_kscale(k):
    if not WIDE:
        return np.ones(k)
    levels = np.array([10, -10, 5, -5, 0])
    a = np.random.permutation(np.resize(levels, k // 512 * 4)).reshape(k // 512, 4)
    idx = np.arange(k)
    return np.exp2(a[idx // 512, idx % 128 // 32])


BF16 = ml_dtypes.bfloat16


def bf(x):
    return np.asarray(x, np.float32).astype(BF16)


def f64(x):
    return np.asarray(x).astype(np.float64)


B, T, D, H, DK, ROPE, NOPE, VD, KVR, QR = 1, 1024, 2048, 16, 128, 64, 64, 128, 512, 1024
EPS = 1.1920928955078125e-07
HALF = ROPE // 2


def rms_norm(h, w):
    var = np.mean(h * h, axis=-1, keepdims=True)
    return h * (1.0 / np.sqrt(var + EPS)) * w


def rope(v):
    inv_freq = 1.0 / (10000.0 ** (f64(np.arange(0, ROPE, 2)) / ROPE))
    freqs = np.outer(f64(np.arange(v.shape[-2])), inv_freq)
    cos, sin = np.cos(freqs), np.sin(freqs)
    v1, v2 = v[..., :HALF], v[..., HALF:]
    return np.concatenate([v1 * cos - v2 * sin, v1 * sin + v2 * cos], axis=-1)


def setup_inputs():
    s, t = mx_kscale(D), mx_kscale(KVR)
    return {'x': bf(np.random.standard_normal((B, T, D)) * s),
            'wkv_c': bf(np.random.standard_normal((D, KVR)) / np.sqrt(D) / s[:, None]),
            'kv_a_norm_w': bf((1.0 + 0.1 * np.random.standard_normal(KVR)) * t),
            'wkv_b': bf(np.random.standard_normal((KVR, H * (NOPE + VD))) / np.sqrt(KVR) / t[:, None]),
            'k_pe': bf(np.random.standard_normal((B, T, ROPE)))}


def reference(x, wkv_c, kv_a_norm_w, wkv_b, k_pe):
    c = mxq(f64(x), 2, 'e4m3') @ mxq(f64(wkv_c), 0, 'e4m3')
    cn = rms_norm(c, f64(kv_a_norm_w))
    kv = mxq(cn, 2, 'e4m3') @ mxq(f64(wkv_b), 0, 'e4m3')
    kv = kv.reshape(B, T, H, NOPE + VD).transpose(0, 2, 1, 3)
    k_nope, v = kv[..., :NOPE], kv[..., NOPE:]
    k_rot = rope(f64(k_pe)[:, None])
    k_rot = np.broadcast_to(k_rot, (B, H, T, ROPE))
    ks = np.concatenate([k_nope, k_rot], axis=-1)
    return ks, np.ascontiguousarray(v)

@@ -1,0 +1,421 @@
+import math
+from contextlib import ExitStack
+
+import concourse.mybir as mybir
+from concourse.masks import make_identity
+
+F32 = mybir.dt.float32
+BF16 = mybir.dt.bfloat16
+I32 = mybir.dt.int32
+U32 = mybir.dt.uint32
+U8 = mybir.dt.uint8
+FP8X4 = mybir.dt.float8_e4m3fn_x4
+ALU = mybir.AluOpType
+ACT = mybir.ActivationFunctionType
+
+P = 128
+PACK = 4
+K_PASS = P * PACK
+
+T, D, KVR, H, NOPE, VD, ROPE = 1024, 2048, 512, 16, 64, 128, 64
+HALF_ROPE = ROPE // 2
+ROPE_BASE = 10000.0
+EPS = 2.0 ** -23
+
+TOK_TILES = T // P
+X_PASSES = D // K_PASS
+HEAD_COLS = NOPE + VD
+GROUP = 4
+GROUPS = H // GROUP
+HALVES = 2
+HALF_TILES = TOK_TILES // HALVES
+
+TWO_PI = 2.0 * math.pi
+TWO_PI_HI = 6.28125
+TWO_PI_LO = TWO_PI - TWO_PI_HI
+
+FLOPS = 2 * T * D * KVR + 2 * T * KVR * H * HEAD_COLS
+
+
+def tile_deepseekmultiheadattention_pb_kernel(
+    tc, x, wkv_c, kv_a_norm_w, wkv_b, k_pe, out_0, out_1
+):
+    nc = tc.nc
+    with ExitStack() as ctx:
+        const = ctx.enter_context(tc.tile_pool(name="const", bufs=1))
+        keep = ctx.enter_context(tc.tile_pool(name="keep", bufs=1))
+        work = ctx.enter_context(tc.tile_pool(name="work", bufs=2))
+        psum = ctx.enter_context(tc.psum_pool(name="psum", bufs=8))
+
+        x_view = x.rearrange("b (p i) k -> p (b i) k", i=TOK_TILES)
+        wb_view = wkv_b.rearrange("(p t) n -> p t n", t=PACK)
+        ks_view = out_0.rearrange("b h (p i) d -> p (b h) i d", i=TOK_TILES)
+        v_view = out_1.rearrange("b h (p i) d -> p (b h) i d", i=TOK_TILES)
+
+        gain_row = const.tile([P, KVR], BF16, name="gain_row")
+        nc.vector.memset(gain_row[:], 0.0)
+        nc.sync.dma_start(
+            out=gain_row[0:1, :], in_=kv_a_norm_w.rearrange("(o n) -> o n", o=1)
+        )
+        kp = const.tile([P, TOK_TILES, 2, HALF_ROPE], BF16, name="kp")
+        nc.sync.dma_start(
+            out=kp[:],
+            in_=k_pe.rearrange("b (p i) (s j) -> p (b i) s j", i=TOK_TILES, s=2),
+        )
+
+        x_pairs = [
+            keep.tile([P, 2, D], BF16, name="x_pair%d" % j) for j in range(TOK_TILES // 2)
+        ]
+        wc_raw = [
+            keep.tile([P, PACK, KVR], BF16, name="wc_raw%d" % g) for g in range(X_PASSES)
+        ]
+        wb_raw = [
+            keep.tile([P, PACK, GROUP * HEAD_COLS], BF16, name="wb_raw%d" % m)
+            for m in range(GROUPS)
+        ]
+
+        def load_x_pair(j):
+            nc.sync.dma_start(out=x_pairs[j][:], in_=x_view[:, 2 * j : 2 * j + 2, :])
+
+        def load_wb(m):
+            cols = slice(GROUP * HEAD_COLS * m, GROUP * HEAD_COLS * (m + 1))
+            nc.sync.dma_start(out=wb_raw[m][:], in_=wb_view[:, :, cols])
+
+        for g in range(X_PASSES):
+            nc.sync.dma_start(
+                out=wc_raw[g][:].rearrange("q (u e) c -> q u (e c)", u=2),
+                in_=wkv_c[K_PASS * g : K_PASS * (g + 1), :].rearrange(
+                    "(u q e) c -> q u (e c)", u=2, e=2
+                ),
+            )
+        load_x_pair(0)
+        load_x_pair(1)
+        load_wb(0)
+        load_x_pair(2)
+        load_x_pair(3)
+        for m in range(1, GROUPS):
+            load_wb(m)
+
+        ones = const.tile([P, P], BF16, name="ones")
+        nc.vector.memset(ones[:], 1.0)
+
+        pos = const.tile([P, TOK_TILES], F32, name="pos")
+        nc.gpsimd.iota(
+            pos[:],
+            pattern=[[1, TOK_TILES]],
+            base=0,
+            channel_multiplier=TOK_TILES,
+            allow_small_or_imprecise_dtypes=True,
+        )
+        ident_f32 = const.tile([P, P], F32, name="ident_f32")
+        make_identity(nc, ident_f32[:])
+        ident_bf16 = const.tile([P, P], BF16, name="ident_bf16")
+        make_identity(nc, ident_bf16[:])
+        angle = const.tile([P, TOK_TILES, HALF_ROPE], F32, name="angle")
+        nc.vector.tensor_copy(out=angle[:, :, 0], in_=pos[:])
+        for step in range(5):
+            width = 2 ** step
+            nc.vector.tensor_scalar_mul(
+                out=angle[:, :, width : 2 * width],
+                in0=angle[:, :, 0:width],
+                scalar1=ROPE_BASE ** (-width / HALF_ROPE),
+            )
+        angle_flat = angle[:].rearrange("p i j -> p (i j)")
+        n_angles = TOK_TILES * HALF_ROPE
+        turns = const.tile([P, n_angles], I32, name="turns")
+        nc.vector.tensor_scalar(
+            out=turns[:], in0=angle_flat, scalar1=1.0 / TWO_PI, scalar2=None, op0=ALU.mult
+        )
+        coarse = const.tile([P, n_angles], F32, name="coarse")
+        nc.vector.scalar_tensor_tensor(
+            out=coarse[:], in0=turns[:], scalar=-TWO_PI_HI, in1=angle_flat,
+            op0=ALU.mult, op1=ALU.add,
+        )
+        phase = const.tile([P, 2, n_angles], F32, name="phase")
+        nc.vector.scalar_tensor_tensor(
+            out=phase[:, 0, :], in0=turns[:], scalar=-TWO_PI_LO, in1=coarse[:],
+            op0=ALU.mult, op1=ALU.add,
+        )
+        nc.vector.tensor_scalar_add(
+            out=phase[:, 1, :], in0=phase[:, 0, :], scalar1=math.pi / 2.0
+        )
+        wrap = const.tile([P, 2, n_angles], F32, name="wrap")
+        nc.vector.tensor_scalar(
+            out=wrap[:], in0=phase[:], scalar1=math.pi, scalar2=-TWO_PI,
+            op0=ALU.is_gt, op1=ALU.mult,
+        )
+        nc.vector.tensor_add(out=phase[:], in0=phase[:], in1=wrap[:])
+        sin_cos = const.tile([P, 2, TOK_TILES, HALF_ROPE], F32, name="sin_cos")
+        nc.scalar.activation(
+            out=sin_cos[:].rearrange("p s i j -> p s (i j)"), in_=phase[:], func=ACT.Sin
+        )
+
+        both = [P, TOK_TILES, 2, HALF_ROPE]
+        by_sin = const.tile(both, F32, name="by_sin")
+        by_cos = const.tile(both, F32, name="by_cos")
+        nc.gpsimd.tensor_tensor(
+            out=by_sin[:], in0=kp[:], in1=sin_cos[:, 0].unsqueeze(2).to_broadcast(both),
+            op=ALU.mult,
+        )
+        nc.gpsimd.tensor_tensor(
+            out=by_cos[:], in0=kp[:], in1=sin_cos[:, 1].unsqueeze(2).to_broadcast(both),
+            op=ALU.mult,
+        )
+
+        ks_stage = [
+            [
+                keep.tile(
+                    [P, GROUP, HALF_TILES, NOPE + ROPE], F32, name="ks_stage%d%d" % (half, b)
+                )
+                for b in range(2)
+            ]
+            for half in range(HALVES)
+        ]
+
+        def fill_rope(stage, half):
+            toks = slice(HALF_TILES * half, HALF_TILES * (half + 1))
+            shape = [P, GROUP, HALF_TILES, HALF_ROPE]
+            nc.gpsimd.tensor_tensor(
+                out=stage[:, :, :, NOPE : NOPE + HALF_ROPE],
+                in0=by_cos[:, toks, 0, :].unsqueeze(1).to_broadcast(shape),
+                in1=by_sin[:, toks, 1, :].unsqueeze(1).to_broadcast(shape),
+                op=ALU.subtract,
+            )
+            nc.gpsimd.tensor_tensor(
+                out=stage[:, :, :, NOPE + HALF_ROPE :],
+                in0=by_sin[:, toks, 0, :].unsqueeze(1).to_broadcast(shape),
+                in1=by_cos[:, toks, 1, :].unsqueeze(1).to_broadcast(shape),
+                op=ALU.add,
+            )
+
+        for half in range(HALVES):
+            for b in range(2):
+                fill_rope(ks_stage[half][b], half)
+
+        gain = const.tile([P, PACK, P], F32, name="gain")
+
+        def spread_gain():
+            gain_ps = psum.tile([P, KVR], F32, tag="bank", name="gain_ps")
+            nc.tensor.matmul(gain_ps[:], lhsT=ones[:], rhs=gain_row[:], start=True, stop=True)
+            nc.vector.tensor_copy(
+                out=gain[:], in_=gain_ps[:].rearrange("p (q t) -> p t q", t=PACK)
+            )
+
+        def codes_and_scales(name, width):
+            codes = keep.tile([P, width], U32, name=name + "_codes", align_bytes=64)
+            scales = keep.tile([P, width], U8, name=name + "_scales", align_bytes=64)
+            return codes, scales
+
+        x_q = [codes_and_scales("x%d" % i, X_PASSES * P) for i in range(TOK_TILES)]
+        wc_q = [codes_and_scales("wc%d" % g, KVR) for g in range(X_PASSES)]
+        cn_q = [codes_and_scales("cn%d" % i, P) for i in range(TOK_TILES)]
+        wv_q = [codes_and_scales("wv%d" % m, GROUP * VD) for m in range(GROUPS)]
+        wk_q = [codes_and_scales("wk%d" % m, GROUP * NOPE) for m in range(GROUPS)]
+
+        def quantise(grouped, pair):
+            codes, scales = pair
+            nc.vector.quantize_mx(
+                out=codes[:].bitcast(FP8X4), scales=scales[:], in_=grouped
+            )
+
+        def mx(out, lhs, lhs_cols, rhs, start, stop):
+            nc.tensor.matmul_mx(
+                out=out,
+                lhsT=lhs[0][:, lhs_cols].bitcast(FP8X4),
+                lhsT_scale=lhs[1][:, lhs_cols],
+                rhs=rhs[0][:].bitcast(FP8X4),
+                rhs_scale=rhs[1][:],
+                start=start,
+                stop=stop,
+            )
+
+        def leave_psum(which, out, in_):
+            if which % 2 == 0:
+                nc.scalar.copy(out=out, in_=in_)
+            else:
+                nc.vector.tensor_copy(out=out, in_=in_)
+
+        x_grouped = {}
+        cn_rows = {}
+
+        def transpose_x(i):
+            words = x_pairs[i // 2][:, i % 2, :].bitcast(F32)
+            grouped = work.tile(
+                [P, X_PASSES * P * PACK], BF16, tag="grouped", bufs=4, align_bytes=64,
+                name="x_grouped",
+            )
+            grouped_words = grouped[:].bitcast(F32)
+            for bank in range(2):
+                xt = psum.tile([P, 4, P], F32, tag="bank", name="xt")
+                for s in range(4):
+                    chunk = 4 * bank + s
+                    nc.tensor.transpose(
+                        xt[:, s, :], words[:, P * chunk : P * (chunk + 1)], ident_f32[:]
+                    )
+                leave_psum(
+                    bank,
+                    grouped_words[:, 512 * bank : 512 * (bank + 1)].rearrange(
+                        "p (g r u) -> p g r u", g=2, u=2
+                    ),
+                    xt[:].rearrange("p (g u) r -> p g r u", u=2),
+                )
+            x_grouped[i] = grouped
+
+        def quantise_x(i):
+            quantise(x_grouped[i][:], x_q[i])
+
+        def project(i):
+            acc = psum.tile([P, KVR], F32, tag="bank", name="acc")
+            for g in range(X_PASSES):
+                mx(acc[:], x_q[i], slice(P * g, P * (g + 1)), wc_q[g],
+                   g == 0, g == X_PASSES - 1)
+            squares = work.tile([P, KVR], BF16, tag="squares", name="squares")
+            mean_sq = work.tile([P, 1], F32, tag="mean_sq", name="mean_sq")
+            nc.scalar.activation(
+                out=squares[:], in_=acc[:], func=ACT.Square,
+                scale=1.0 / math.sqrt(KVR), accum_out=mean_sq[:],
+            )
+            rms = work.tile([P, 1], F32, tag="rms", name="rms")
+            nc.scalar.activation(out=rms[:], in_=mean_sq[:], func=ACT.Sqrt, bias=EPS)
+            inv_rms = work.tile([P, 1], F32, tag="inv_rms", name="inv_rms")
+            nc.vector.reciprocal(out=inv_rms[:], in_=rms[:])
+            cn = work.tile([P, PACK, P], BF16, tag="cn", bufs=4, name="cn")
+            nc.vector.scalar_tensor_tensor(
+                out=cn[:],
+                in0=acc[:].rearrange("p (q t) -> p t q", t=PACK),
+                scalar=inv_rms[:, 0:1],
+                in1=gain[:],
+                op0=ALU.mult,
+                op1=ALU.mult,
+            )
+            cn_rows[i] = cn
+
+        def transpose_cn(i):
+            cn_t = psum.tile([P, PACK, P], BF16, tag="bank", name="cn_t")
+            for t in range(PACK):
+                nc.tensor.transpose(cn_t[:, t, :], cn_rows[i][:, t, :], ident_bf16[:])
+            grouped = work.tile(
+                [P, P, PACK], BF16, tag="cn_grouped", align_bytes=64, name="cn_grouped"
+            )
+            nc.scalar.copy(out=grouped[:], in_=cn_t[:].rearrange("p t r -> p r t"))
+            quantise(grouped[:].rearrange("p r t -> p (r t)"), cn_q[i])
+
+        def grouped_columns(width):
+            grouped = work.tile(
+                [P, X_PASSES * P * PACK], BF16, tag="grouped", bufs=4, align_bytes=64,
+                name="w_grouped",
+            )
+            return grouped[:, 0 : width * PACK]
+
+        def regroup_wc(g):
+            flat = grouped_columns(KVR)
+            dst = flat.rearrange("p (c t) -> p c t", t=PACK)
+            src = wc_raw[g][:].rearrange("p t c -> p c t")
+            nc.scalar.copy(out=dst[:, 0 : KVR // 2, :], in_=src[:, 0 : KVR // 2, :])
+            nc.vector.tensor_copy(out=dst[:, KVR // 2 :, :], in_=src[:, KVR // 2 :, :])
+            return flat
+
+        def regroup_wb(m, first, width):
+            flat = grouped_columns(GROUP * width)
+            heads = wb_raw[m][:].rearrange("p t (h f) -> p t h f", f=HEAD_COLS)
+            nc.vector.tensor_copy(
+                out=flat.rearrange("p (h d t) -> p h d t", h=GROUP, t=PACK),
+                in_=heads[:, :, :, first : first + width].rearrange("p t h d -> p h d t"),
+            )
+            return flat
+
+        def vector_takes(half, n):
+            if half == 0:
+                return 1 if n % 4 == 3 else 0
+            return n % 2
+
+        def v_unit(m, half):
+            stage = work.tile([P, GROUP, HALF_TILES, VD], F32, tag="v_stage", bufs=4,
+                              name="v_stage")
+            for s in range(HALF_TILES):
+                i = HALF_TILES * half + s
+                kv = psum.tile([P, GROUP * VD], F32, tag="bank", name="kv")
+                mx(kv[:], cn_q[i], slice(0, P), wv_q[m], True, True)
+                leave_psum(
+                    vector_takes(half, s),
+                    stage[:, :, s, :],
+                    kv[:].rearrange("p (h d) -> p h d", h=GROUP),
+                )
+            nc.sync.dma_start(
+                out=v_view[:, GROUP * m : GROUP * (m + 1),
+                           HALF_TILES * half : HALF_TILES * (half + 1), :],
+                in_=stage[:],
+            )
+
+        def k_unit(m, half):
+            stage = ks_stage[half][m % 2]
+            for pair in range(HALF_TILES // 2):
+                kk = psum.tile([P, 2, GROUP * NOPE], F32, tag="bank", name="kk")
+                for s in range(2):
+                    i = HALF_TILES * half + 2 * pair + s
+                    mx(kk[:, s, :], cn_q[i], slice(0, P), wk_q[m], True, True)
+                leave_psum(
+                    vector_takes(half, 2 + pair),
+                    stage[:, :, 2 * pair : 2 * pair + 2, 0:NOPE].rearrange("p h i d -> p i h d"),
+                    kk[:].rearrange("p i (h d) -> p i h d", h=GROUP),
+                )
+            nc.sync.dma_start(
+                out=ks_view[:, GROUP * m : GROUP * (m + 1),
+                            HALF_TILES * half : HALF_TILES * (half + 1), :],
+                in_=stage[:],
+            )
+
+        def unit(u, half):
+            if u % 2 == 0:
+                v_unit(u // 2, half)
+            else:
+                k_unit(u // 2, half)
+
+        def prepare_unit_weights(u):
+            if u % 2 == 0:
+                quantise(regroup_wb(u // 2, NOPE, VD), wv_q[u // 2])
+            else:
+                quantise(regroup_wb(u // 2, 0, NOPE), wk_q[u // 2])
+
+        def transpose_half(half):
+            first = HALF_TILES * half
+            for i in range(first, first + HALF_TILES):
+                transpose_x(i)
+                if i > first:
+                    quantise_x(i - 1)
+            quantise_x(first + HALF_TILES - 1)
+
+        def unit_with_weights(u):
+            prepare_unit_weights(u)
+            unit(u, 0)
+
+        units = 2 * GROUPS
+
+        flats = {}
+        for g in range(X_PASSES):
+            flats[g] = regroup_wc(g)
+            if g > 0:
+                quantise(flats[g - 1], wc_q[g - 1])
+        quantise(flats[X_PASSES - 1], wc_q[X_PASSES - 1])
+
+        transpose_half(0)
+        spread_gain()
+        prepare_unit_weights(0)
+        for i in range(HALF_TILES):
+            project(i)
+        for i in range(HALF_TILES):
+            transpose_cn(i)
+
+        unit(0, 0)
+        unit_with_weights(1)
+        transpose_half(1)
+        for s in range(HALF_TILES):
+            unit_with_weights(2 + s)
+            project(HALF_TILES + s)
+        unit_with_weights(6)
+        for i in range(HALF_TILES, TOK_TILES):
+            transpose_cn(i)
+        unit_with_weights(7)
+
+        for u in range(units):
+            unit(u, 1)

@@ -16,6 +16,7 @@ ACT = mybir.ActivationFunctionType
 P = 128
 PACK = 4
 K_PASS = P * PACK
+RUN = 4
 
 T, D, KVR, H, NOPE, VD, ROPE = 1024, 2048, 512, 16, 64, 128, 64
 HALF_ROPE = ROPE // 2
@@ -46,6 +47,7 @@ def tile_deepseekmultiheadattention_pb_kernel(
         keep = ctx.enter_context(tc.tile_pool(name="keep", bufs=1))
         work = ctx.enter_context(tc.tile_pool(name="work", bufs=2))
         psum = ctx.enter_context(tc.psum_pool(name="psum", bufs=8))
+        ctx.enter_context(tc.manual_schedule())
 
         x_view = x.rearrange("b (p i) k -> p (b i) k", i=TOK_TILES)
         wb_view = wkv_b.rearrange("(p t) n -> p t n", t=PACK)
@@ -253,7 +255,7 @@ def tile_deepseekmultiheadattention_pb_kernel(
                         xt[:, s, :], words[:, P * chunk : P * (chunk + 1)], ident_f32[:]
                     )
                 leave_psum(
-                    bank,
+                    0,
                     grouped_words[:, 512 * bank : 512 * (bank + 1)].rearrange(
                         "p (g r u) -> p g r u", g=2, u=2
                     ),
@@ -309,18 +311,21 @@ def tile_deepseekmultiheadattention_pb_kernel(
 
         def regroup_wc(g):
             flat = grouped_columns(KVR)
-            dst = flat.rearrange("p (c t) -> p c t", t=PACK)
-            src = wc_raw[g][:].rearrange("p t c -> p c t")
-            nc.scalar.copy(out=dst[:, 0 : KVR // 2, :], in_=src[:, 0 : KVR // 2, :])
-            nc.vector.tensor_copy(out=dst[:, KVR // 2 :, :], in_=src[:, KVR // 2 :, :])
+            dst = flat.rearrange("p (c i t) -> p c t i", i=RUN, t=PACK)
+            src = wc_raw[g][:].rearrange("p t (c i) -> p c t i", i=RUN)
+            middle = KVR // RUN // 2
+            nc.scalar.copy(out=dst[:, 0:middle], in_=src[:, 0:middle])
+            nc.vector.tensor_copy(out=dst[:, middle:], in_=src[:, middle:])
             return flat
 
         def regroup_wb(m, first, width):
             flat = grouped_columns(GROUP * width)
             heads = wb_raw[m][:].rearrange("p t (h f) -> p t h f", f=HEAD_COLS)
             nc.vector.tensor_copy(
-                out=flat.rearrange("p (h d t) -> p h d t", h=GROUP, t=PACK),
-                in_=heads[:, :, :, first : first + width].rearrange("p t h d -> p h d t"),
+                out=flat.rearrange("p (h c i t) -> p h c t i", h=GROUP, i=RUN, t=PACK),
+                in_=heads[:, :, :, first : first + width].rearrange(
+                    "p t h (c i) -> p h c t i", i=RUN
+                ),
             )
             return flat
 
@@ -371,26 +376,21 @@ def tile_deepseekmultiheadattention_pb_kernel(
             else:
                 k_unit(u // 2, half)
 
-        def prepare_unit_weights(u):
+        unit_flats = {}
+
+        def regroup_unit(u):
             if u % 2 == 0:
-                quantise(regroup_wb(u // 2, NOPE, VD), wv_q[u // 2])
+                unit_flats[u] = regroup_wb(u // 2, NOPE, VD)
             else:
-                quantise(regroup_wb(u // 2, 0, NOPE), wk_q[u // 2])
+                unit_flats[u] = regroup_wb(u // 2, 0, NOPE)
 
-        def transpose_half(half):
-            first = HALF_TILES * half
-            for i in range(first, first + HALF_TILES):
-                transpose_x(i)
-                if i > first:
-                    quantise_x(i - 1)
-            quantise_x(first + HALF_TILES - 1)
-
-        def unit_with_weights(u):
-            prepare_unit_weights(u)
-            unit(u, 0)
+        def quantise_unit(u):
+            quantise(unit_flats[u], wv_q[u // 2] if u % 2 == 0 else wk_q[u // 2])
 
         units = 2 * GROUPS
+        second = HALF_TILES
 
+        spread_gain()
         flats = {}
         for g in range(X_PASSES):
             flats[g] = regroup_wc(g)
@@ -398,24 +398,34 @@ def tile_deepseekmultiheadattention_pb_kernel(
                 quantise(flats[g - 1], wc_q[g - 1])
         quantise(flats[X_PASSES - 1], wc_q[X_PASSES - 1])
 
-        transpose_half(0)
-        spread_gain()
-        prepare_unit_weights(0)
+        for i in range(HALF_TILES):
+            transpose_x(i)
+        quantise_x(0)
+        quantise_x(1)
+        regroup_unit(0)
+        quantise_x(2)
+        quantise_x(3)
+        quantise_unit(0)
         for i in range(HALF_TILES):
             project(i)
         for i in range(HALF_TILES):
             transpose_cn(i)
+        regroup_unit(1)
 
-        unit(0, 0)
-        unit_with_weights(1)
-        transpose_half(1)
-        for s in range(HALF_TILES):
-            unit_with_weights(2 + s)
-            project(HALF_TILES + s)
-        unit_with_weights(6)
-        for i in range(HALF_TILES, TOK_TILES):
-            transpose_cn(i)
-        unit_with_weights(7)
+        for u in range(units):
+            if u + 1 < units:
+                quantise_unit(u + 1)
+            unit(u, 0)
+            if u + 2 < units:
+                regroup_unit(u + 2)
+            if u < HALF_TILES:
+                transpose_x(second + u)
+            if 1 <= u < HALF_TILES + 1:
+                quantise_x(second + u - 1)
+            if 2 <= u < HALF_TILES + 2:
+                project(second + u - 2)
+            if u >= HALF_TILES:
+                transpose_cn(u)
 
         for u in range(units):
             unit(u, 1)

@@ -100,6 +100,8 @@ def tile_deepseekmultiheadattention_pb_kernel(
 
         ones = const.tile([P, P], BF16, name="ones")
         nc.vector.memset(ones[:], 1.0)
+        table_warmer = const.tile([P, 1], F32, name="table_warmer")
+        nc.vector.memset(table_warmer[:], 1.0)
 
         pos = const.tile([P, TOK_TILES], F32, name="pos")
         nc.gpsimd.iota(
@@ -151,18 +153,7 @@ def tile_deepseekmultiheadattention_pb_kernel(
         nc.scalar.activation(
             out=sin_cos[:].rearrange("p s i j -> p s (i j)"), in_=phase[:], func=ACT.Sin
         )
-
-        both = [P, TOK_TILES, 2, HALF_ROPE]
-        by_sin = const.tile(both, F32, name="by_sin")
-        by_cos = const.tile(both, F32, name="by_cos")
-        nc.gpsimd.tensor_tensor(
-            out=by_sin[:], in0=kp[:], in1=sin_cos[:, 0].unsqueeze(2).to_broadcast(both),
-            op=ALU.mult,
-        )
-        nc.gpsimd.tensor_tensor(
-            out=by_cos[:], in0=kp[:], in1=sin_cos[:, 1].unsqueeze(2).to_broadcast(both),
-            op=ALU.mult,
-        )
+        nc.scalar.activation(out=table_warmer[:], in_=table_warmer[:], func=ACT.Sqrt)
 
         ks_stage = [
             [
@@ -173,26 +164,39 @@ def tile_deepseekmultiheadattention_pb_kernel(
             ]
             for half in range(HALVES)
         ]
+        both = [P, TOK_TILES, 2, HALF_ROPE]
+        by_sin = const.tile(both, F32, name="by_sin")
+        by_cos = const.tile(both, F32, name="by_cos")
+        rotated = const.tile(both, F32, name="rotated")
 
-        def fill_rope(stage, half):
-            toks = slice(HALF_TILES * half, HALF_TILES * (half + 1))
-            shape = [P, GROUP, HALF_TILES, HALF_ROPE]
-            nc.gpsimd.tensor_tensor(
-                out=stage[:, :, :, NOPE : NOPE + HALF_ROPE],
-                in0=by_cos[:, toks, 0, :].unsqueeze(1).to_broadcast(shape),
-                in1=by_sin[:, toks, 1, :].unsqueeze(1).to_broadcast(shape),
+        def rotate_k_pe():
+            nc.vector.tensor_tensor(
+                out=by_sin[:], in0=kp[:], in1=sin_cos[:, 0].unsqueeze(2).to_broadcast(both),
+                op=ALU.mult,
+            )
+            nc.vector.tensor_tensor(
+                out=by_cos[:], in0=kp[:], in1=sin_cos[:, 1].unsqueeze(2).to_broadcast(both),
+                op=ALU.mult,
+            )
+            nc.vector.tensor_tensor(
+                out=rotated[:, :, 0, :], in0=by_cos[:, :, 0, :], in1=by_sin[:, :, 1, :],
                 op=ALU.subtract,
             )
-            nc.gpsimd.tensor_tensor(
-                out=stage[:, :, :, NOPE + HALF_ROPE :],
-                in0=by_sin[:, toks, 0, :].unsqueeze(1).to_broadcast(shape),
-                in1=by_cos[:, toks, 1, :].unsqueeze(1).to_broadcast(shape),
+            nc.vector.tensor_tensor(
+                out=rotated[:, :, 1, :], in0=by_sin[:, :, 0, :], in1=by_cos[:, :, 1, :],
                 op=ALU.add,
             )
 
-        for half in range(HALVES):
-            for b in range(2):
-                fill_rope(ks_stage[half][b], half)
+        def fill_rope(half):
+            toks = slice(HALF_TILES * half, HALF_TILES * (half + 1))
+            for stage in ks_stage[half]:
+                nc.vector.tensor_copy(
+                    out=stage[:, :, :, NOPE:],
+                    in_=rotated[:, toks, :, :]
+                    .rearrange("p i s j -> p i (s j)")
+                    .unsqueeze(1)
+                    .to_broadcast([P, GROUP, HALF_TILES, ROPE]),
+                )
 
         gain = const.tile([P, PACK, P], F32, name="gain")
 
@@ -397,13 +401,15 @@ def tile_deepseekmultiheadattention_pb_kernel(
             if g > 0:
                 quantise(flats[g - 1], wc_q[g - 1])
         quantise(flats[X_PASSES - 1], wc_q[X_PASSES - 1])
+        rotate_k_pe()
 
         for i in range(HALF_TILES):
             transpose_x(i)
         quantise_x(0)
+        fill_rope(0)
         quantise_x(1)
-        regroup_unit(0)
         quantise_x(2)
+        regroup_unit(0)
         quantise_x(3)
         quantise_unit(0)
         for i in range(HALF_TILES):
@@ -427,5 +433,6 @@ def tile_deepseekmultiheadattention_pb_kernel(
             if u >= HALF_TILES:
                 transpose_cn(u)
 
+        fill_rope(1)
         for u in range(units):
             unit(u, 1)

@@ -28,8 +28,10 @@ X_PASSES = D // K_PASS
 HEAD_COLS = NOPE + VD
 GROUP = 4
 GROUPS = H // GROUP
-HALVES = 2
-HALF_TILES = TOK_TILES // HALVES
+UNITS = 2 * GROUPS
+
+BATCH_TILES = (5, 3)
+BATCH_START = (0, 5)
 
 TWO_PI = 2.0 * math.pi
 TWO_PI_HI = 6.28125
@@ -54,20 +56,13 @@ def tile_deepseekmultiheadattention_pb_kernel(
         ks_view = out_0.rearrange("b h (p i) d -> p (b h) i d", i=TOK_TILES)
         v_view = out_1.rearrange("b h (p i) d -> p (b h) i d", i=TOK_TILES)
 
-        gain_row = const.tile([P, KVR], BF16, name="gain_row")
-        nc.vector.memset(gain_row[:], 0.0)
-        nc.sync.dma_start(
-            out=gain_row[0:1, :], in_=kv_a_norm_w.rearrange("(o n) -> o n", o=1)
-        )
-        kp = const.tile([P, TOK_TILES, 2, HALF_ROPE], BF16, name="kp")
-        nc.sync.dma_start(
-            out=kp[:],
-            in_=k_pe.rearrange("b (p i) (s j) -> p (b i) s j", i=TOK_TILES, s=2),
-        )
+        def batch_tiles(batch):
+            return range(BATCH_START[batch], BATCH_START[batch] + BATCH_TILES[batch])
 
-        x_pairs = [
-            keep.tile([P, 2, D], BF16, name="x_pair%d" % j) for j in range(TOK_TILES // 2)
-        ]
+        def batch_slice(batch):
+            return slice(BATCH_START[batch], BATCH_START[batch] + BATCH_TILES[batch])
+
+        x_rows = [keep.tile([P, D], BF16, name="x_rows%d" % i) for i in range(TOK_TILES)]
         wc_raw = [
             keep.tile([P, PACK, KVR], BF16, name="wc_raw%d" % g) for g in range(X_PASSES)
         ]
@@ -75,9 +70,12 @@ def tile_deepseekmultiheadattention_pb_kernel(
             keep.tile([P, PACK, GROUP * HEAD_COLS], BF16, name="wb_raw%d" % m)
             for m in range(GROUPS)
         ]
+        kp = const.tile([P, TOK_TILES, 2, HALF_ROPE], BF16, name="kp")
+        gain_row = const.tile([P, KVR], BF16, name="gain_row")
+        nc.vector.memset(gain_row[:], 0.0)
 
-        def load_x_pair(j):
-            nc.sync.dma_start(out=x_pairs[j][:], in_=x_view[:, 2 * j : 2 * j + 2, :])
+        def load_x(i):
+            nc.sync.dma_start(out=x_rows[i][:], in_=x_view[:, i, :])
 
         def load_wb(m):
             cols = slice(GROUP * HEAD_COLS * m, GROUP * HEAD_COLS * (m + 1))
@@ -90,11 +88,18 @@ def tile_deepseekmultiheadattention_pb_kernel(
                     "(u q e) c -> q u (e c)", u=2, e=2
                 ),
             )
-        load_x_pair(0)
-        load_x_pair(1)
+        nc.sync.dma_start(
+            out=kp[:],
+            in_=k_pe.rearrange("b (p i) (s j) -> p (b i) s j", i=TOK_TILES, s=2),
+        )
+        nc.sync.dma_start(
+            out=gain_row[0:1, :], in_=kv_a_norm_w.rearrange("(o n) -> o n", o=1)
+        )
+        for i in batch_tiles(0):
+            load_x(i)
         load_wb(0)
-        load_x_pair(2)
-        load_x_pair(3)
+        for i in batch_tiles(1):
+            load_x(i)
         for m in range(1, GROUPS):
             load_wb(m)
 
@@ -158,11 +163,12 @@ def tile_deepseekmultiheadattention_pb_kernel(
         ks_stage = [
             [
                 keep.tile(
-                    [P, GROUP, HALF_TILES, NOPE + ROPE], F32, name="ks_stage%d%d" % (half, b)
+                    [P, GROUP, BATCH_TILES[batch], NOPE + ROPE], F32,
+                    name="ks_stage%d%d" % (batch, b),
                 )
                 for b in range(2)
             ]
-            for half in range(HALVES)
+            for batch in range(2)
         ]
         both = [P, TOK_TILES, 2, HALF_ROPE]
         by_sin = const.tile(both, F32, name="by_sin")
@@ -187,22 +193,22 @@ def tile_deepseekmultiheadattention_pb_kernel(
                 op=ALU.add,
             )
 
-        def fill_rope(half):
-            toks = slice(HALF_TILES * half, HALF_TILES * (half + 1))
-            for stage in ks_stage[half]:
+        def fill_rope(batch):
+            for stage in ks_stage[batch]:
                 nc.vector.tensor_copy(
                     out=stage[:, :, :, NOPE:],
-                    in_=rotated[:, toks, :, :]
+                    in_=rotated[:, batch_slice(batch), :, :]
                     .rearrange("p i s j -> p i (s j)")
                     .unsqueeze(1)
-                    .to_broadcast([P, GROUP, HALF_TILES, ROPE]),
+                    .to_broadcast([P, GROUP, BATCH_TILES[batch], ROPE]),
                 )
 
         gain = const.tile([P, PACK, P], F32, name="gain")
 
-        def spread_gain():
-            gain_ps = psum.tile([P, KVR], F32, tag="bank", name="gain_ps")
-            nc.tensor.matmul(gain_ps[:], lhsT=ones[:], rhs=gain_row[:], start=True, stop=True)
+        gain_ps = psum.tile([P, KVR], F32, tag="bank", name="gain_ps")
+        nc.tensor.matmul(gain_ps[:], lhsT=ones[:], rhs=gain_row[:], start=True, stop=True)
+
+        def keep_gain():
             nc.vector.tensor_copy(
                 out=gain[:], in_=gain_ps[:].rearrange("p (q t) -> p t q", t=PACK)
             )
@@ -245,7 +251,7 @@ def tile_deepseekmultiheadattention_pb_kernel(
         cn_rows = {}
 
         def transpose_x(i):
-            words = x_pairs[i // 2][:, i % 2, :].bitcast(F32)
+            words = x_rows[i][:].bitcast(F32)
             grouped = work.tile(
                 [P, X_PASSES * P * PACK], BF16, tag="grouped", bufs=4, align_bytes=64,
                 name="x_grouped",
@@ -285,7 +291,7 @@ def tile_deepseekmultiheadattention_pb_kernel(
             nc.scalar.activation(out=rms[:], in_=mean_sq[:], func=ACT.Sqrt, bias=EPS)
             inv_rms = work.tile([P, 1], F32, tag="inv_rms", name="inv_rms")
             nc.vector.reciprocal(out=inv_rms[:], in_=rms[:])
-            cn = work.tile([P, PACK, P], BF16, tag="cn", bufs=4, name="cn")
+            cn = work.tile([P, PACK, P], BF16, tag="cn", bufs=max(BATCH_TILES), name="cn")
             nc.vector.scalar_tensor_tensor(
                 out=cn[:],
                 in0=acc[:].rearrange("p (q t) -> p t q", t=PACK),
@@ -333,52 +339,49 @@ def tile_deepseekmultiheadattention_pb_kernel(
             )
             return flat
 
-        def vector_takes(half, n):
-            if half == 0:
+        def vector_takes(batch, n):
+            if batch == 0:
                 return 1 if n % 4 == 3 else 0
             return n % 2
 
-        def v_unit(m, half):
-            stage = work.tile([P, GROUP, HALF_TILES, VD], F32, tag="v_stage", bufs=4,
-                              name="v_stage")
-            for s in range(HALF_TILES):
-                i = HALF_TILES * half + s
+        def v_unit(m, batch):
+            tiles = BATCH_TILES[batch]
+            stage = work.tile([P, GROUP, tiles, VD], F32, tag="v_stage", bufs=3, name="v_stage")
+            for s in range(tiles):
                 kv = psum.tile([P, GROUP * VD], F32, tag="bank", name="kv")
-                mx(kv[:], cn_q[i], slice(0, P), wv_q[m], True, True)
+                mx(kv[:], cn_q[BATCH_START[batch] + s], slice(0, P), wv_q[m], True, True)
                 leave_psum(
-                    vector_takes(half, s),
+                    vector_takes(batch, s),
                     stage[:, :, s, :],
                     kv[:].rearrange("p (h d) -> p h d", h=GROUP),
                 )
             nc.sync.dma_start(
-                out=v_view[:, GROUP * m : GROUP * (m + 1),
-                           HALF_TILES * half : HALF_TILES * (half + 1), :],
-                in_=stage[:],
+                out=v_view[:, GROUP * m : GROUP * (m + 1), batch_slice(batch), :], in_=stage[:]
             )
 
-        def k_unit(m, half):
-            stage = ks_stage[half][m % 2]
-            for pair in range(HALF_TILES // 2):
+        def k_unit(m, batch):
+            tiles = BATCH_TILES[batch]
+            stage = ks_stage[batch][m % 2]
+            for first in range(0, tiles, 2):
+                count = min(2, tiles - first)
                 kk = psum.tile([P, 2, GROUP * NOPE], F32, tag="bank", name="kk")
-                for s in range(2):
-                    i = HALF_TILES * half + 2 * pair + s
-                    mx(kk[:, s, :], cn_q[i], slice(0, P), wk_q[m], True, True)
+                for s in range(count):
+                    mx(kk[:, s, :], cn_q[BATCH_START[batch] + first + s], slice(0, P),
+                       wk_q[m], True, True)
                 leave_psum(
-                    vector_takes(half, 2 + pair),
-                    stage[:, :, 2 * pair : 2 * pair + 2, 0:NOPE].rearrange("p h i d -> p i h d"),
-                    kk[:].rearrange("p i (h d) -> p i h d", h=GROUP),
+                    vector_takes(batch, 2 + first // 2),
+                    stage[:, :, first : first + count, 0:NOPE].rearrange("p h i d -> p i h d"),
+                    kk[:, 0:count, :].rearrange("p i (h d) -> p i h d", h=GROUP),
                 )
             nc.sync.dma_start(
-                out=ks_view[:, GROUP * m : GROUP * (m + 1),
-                            HALF_TILES * half : HALF_TILES * (half + 1), :],
-                in_=stage[:],
+                out=ks_view[:, GROUP * m : GROUP * (m + 1), batch_slice(batch), :], in_=stage[:]
             )
 
-        def unit(u, half):
+        def unit(u, batch):
             if u % 2 == 0:
-                v_unit(u // 2, half)
+                v_unit(u // 2, batch)
             else:
-                k_unit(u // 2, half)
+                k_unit(u // 2, batch)
 
         unit_flats = {}
 
@@ -391,48 +394,49 @@ def tile_deepseekmultiheadattention_pb_kernel(
         def quantise_unit(u):
             quantise(unit_flats[u], wv_q[u // 2] if u % 2 == 0 else wk_q[u // 2])
 
-        units = 2 * GROUPS
-        second = HALF_TILES
-
-        spread_gain()
         flats = {}
         for g in range(X_PASSES):
             flats[g] = regroup_wc(g)
             if g > 0:
                 quantise(flats[g - 1], wc_q[g - 1])
-        quantise(flats[X_PASSES - 1], wc_q[X_PASSES - 1])
         rotate_k_pe()
+        quantise(flats[X_PASSES - 1], wc_q[X_PASSES - 1])
 
-        for i in range(HALF_TILES):
+        for i in batch_tiles(0):
             transpose_x(i)
-        quantise_x(0)
-        fill_rope(0)
-        quantise_x(1)
-        quantise_x(2)
-        regroup_unit(0)
-        quantise_x(3)
-        quantise_unit(0)
-        for i in range(HALF_TILES):
+            if i == 1:
+                keep_gain()
+            if i > 0:
+                quantise_x(i - 1)
+        quantise_x(BATCH_TILES[0] - 1)
+        for i in batch_tiles(0):
             project(i)
-        for i in range(HALF_TILES):
+            if i == 0:
+                regroup_unit(0)
+        quantise_unit(0)
+        for i in batch_tiles(0):
             transpose_cn(i)
         regroup_unit(1)
 
-        for u in range(units):
-            if u + 1 < units:
+        second = BATCH_START[1]
+        tiles = BATCH_TILES[1]
+        for u in range(UNITS):
+            if u + 1 < UNITS:
                 quantise_unit(u + 1)
             unit(u, 0)
-            if u + 2 < units:
+            if u == 0:
+                fill_rope(0)
+            if u + 2 < UNITS:
                 regroup_unit(u + 2)
-            if u < HALF_TILES:
+            if u < tiles:
                 transpose_x(second + u)
-            if 1 <= u < HALF_TILES + 1:
+            if 1 <= u < tiles + 1:
                 quantise_x(second + u - 1)
-            if 2 <= u < HALF_TILES + 2:
+            if 2 <= u < tiles + 2:
                 project(second + u - 2)
-            if u >= HALF_TILES:
-                transpose_cn(u)
+            if 4 <= u < tiles + 4:
+                transpose_cn(second + u - 4)
 
         fill_rope(1)
-        for u in range(units):
+        for u in range(UNITS):
             unit(u, 1)

import math
from contextlib import ExitStack

import concourse.mybir as mybir
from concourse.masks import make_identity

F32 = mybir.dt.float32
BF16 = mybir.dt.bfloat16
I32 = mybir.dt.int32
U32 = mybir.dt.uint32
U8 = mybir.dt.uint8
FP8X4 = mybir.dt.float8_e4m3fn_x4
ALU = mybir.AluOpType
ACT = mybir.ActivationFunctionType

P = 128
PACK = 4
K_PASS = P * PACK
RUN = 4

T, D, KVR, H, NOPE, VD, ROPE = 1024, 2048, 512, 16, 64, 128, 64
HALF_ROPE = ROPE // 2
ROPE_BASE = 10000.0
EPS = 2.0 ** -23

TOK_TILES = T // P
X_PASSES = D // K_PASS
HEAD_COLS = NOPE + VD
GROUP = 4
GROUPS = H // GROUP
UNITS = 2 * GROUPS

BATCH_TILES = (5, 3)
BATCH_START = (0, 5)

TWO_PI = 2.0 * math.pi
TWO_PI_HI = 6.28125
TWO_PI_LO = TWO_PI - TWO_PI_HI

FLOPS = 2 * T * D * KVR + 2 * T * KVR * H * HEAD_COLS


def tile_deepseekmultiheadattention_pb_kernel(
    tc, x, wkv_c, kv_a_norm_w, wkv_b, k_pe, out_0, out_1
):
    nc = tc.nc
    with ExitStack() as ctx:
        const = ctx.enter_context(tc.tile_pool(name="const", bufs=1))
        keep = ctx.enter_context(tc.tile_pool(name="keep", bufs=1))
        work = ctx.enter_context(tc.tile_pool(name="work", bufs=2))
        psum = ctx.enter_context(tc.psum_pool(name="psum", bufs=8))
        ctx.enter_context(tc.manual_schedule())

        x_view = x.rearrange("b (p i) k -> p (b i) k", i=TOK_TILES)
        wb_view = wkv_b.rearrange("(p t) n -> p t n", t=PACK)
        ks_view = out_0.rearrange("b h (p i) d -> p (b h) i d", i=TOK_TILES)
        v_view = out_1.rearrange("b h (p i) d -> p (b h) i d", i=TOK_TILES)

        def batch_tiles(batch):
            return range(BATCH_START[batch], BATCH_START[batch] + BATCH_TILES[batch])

        def batch_slice(batch):
            return slice(BATCH_START[batch], BATCH_START[batch] + BATCH_TILES[batch])

        x_rows = [keep.tile([P, D], BF16, name="x_rows%d" % i) for i in range(TOK_TILES)]
        wc_raw = [
            keep.tile([P, PACK, KVR], BF16, name="wc_raw%d" % g) for g in range(X_PASSES)
        ]
        wb_raw = [
            keep.tile([P, PACK, GROUP * HEAD_COLS], BF16, name="wb_raw%d" % m)
            for m in range(GROUPS)
        ]
        kp = const.tile([P, TOK_TILES, 2, HALF_ROPE], BF16, name="kp")
        gain_row = const.tile([P, KVR], BF16, name="gain_row")
        nc.vector.memset(gain_row[:], 0.0)

        def load_x(i):
            nc.sync.dma_start(out=x_rows[i][:], in_=x_view[:, i, :])

        def load_wb(m):
            cols = slice(GROUP * HEAD_COLS * m, GROUP * HEAD_COLS * (m + 1))
            nc.sync.dma_start(out=wb_raw[m][:], in_=wb_view[:, :, cols])

        for g in range(X_PASSES):
            nc.sync.dma_start(
                out=wc_raw[g][:].rearrange("q (u e) c -> q u (e c)", u=2),
                in_=wkv_c[K_PASS * g : K_PASS * (g + 1), :].rearrange(
                    "(u q e) c -> q u (e c)", u=2, e=2
                ),
            )
        nc.sync.dma_start(
            out=kp[:],
            in_=k_pe.rearrange("b (p i) (s j) -> p (b i) s j", i=TOK_TILES, s=2),
        )
        nc.sync.dma_start(
            out=gain_row[0:1, :], in_=kv_a_norm_w.rearrange("(o n) -> o n", o=1)
        )
        for i in batch_tiles(0):
            load_x(i)
        load_wb(0)
        for i in batch_tiles(1):
            load_x(i)
        for m in range(1, GROUPS):
            load_wb(m)

        ones = const.tile([P, P], BF16, name="ones")
        nc.vector.memset(ones[:], 1.0)
        table_warmer = const.tile([P, 1], F32, name="table_warmer")
        nc.vector.memset(table_warmer[:], 1.0)

        pos = const.tile([P, TOK_TILES], F32, name="pos")
        nc.gpsimd.iota(
            pos[:],
            pattern=[[1, TOK_TILES]],
            base=0,
            channel_multiplier=TOK_TILES,
            allow_small_or_imprecise_dtypes=True,
        )
        ident_f32 = const.tile([P, P], F32, name="ident_f32")
        make_identity(nc, ident_f32[:])
        ident_bf16 = const.tile([P, P], BF16, name="ident_bf16")
        make_identity(nc, ident_bf16[:])
        angle = const.tile([P, TOK_TILES, HALF_ROPE], F32, name="angle")
        nc.vector.tensor_copy(out=angle[:, :, 0], in_=pos[:])
        for step in range(5):
            width = 2 ** step
            nc.vector.tensor_scalar_mul(
                out=angle[:, :, width : 2 * width],
                in0=angle[:, :, 0:width],
                scalar1=ROPE_BASE ** (-width / HALF_ROPE),
            )
        angle_flat = angle[:].rearrange("p i j -> p (i j)")
        n_angles = TOK_TILES * HALF_ROPE
        turns = const.tile([P, n_angles], I32, name="turns")
        nc.vector.tensor_scalar(
            out=turns[:], in0=angle_flat, scalar1=1.0 / TWO_PI, scalar2=None, op0=ALU.mult
        )
        coarse = const.tile([P, n_angles], F32, name="coarse")
        nc.vector.scalar_tensor_tensor(
            out=coarse[:], in0=turns[:], scalar=-TWO_PI_HI, in1=angle_flat,
            op0=ALU.mult, op1=ALU.add,
        )
        phase = const.tile([P, 2, n_angles], F32, name="phase")
        nc.vector.scalar_tensor_tensor(
            out=phase[:, 0, :], in0=turns[:], scalar=-TWO_PI_LO, in1=coarse[:],
            op0=ALU.mult, op1=ALU.add,
        )
        nc.vector.tensor_scalar_add(
            out=phase[:, 1, :], in0=phase[:, 0, :], scalar1=math.pi / 2.0
        )
        wrap = const.tile([P, 2, n_angles], F32, name="wrap")
        nc.vector.tensor_scalar(
            out=wrap[:], in0=phase[:], scalar1=math.pi, scalar2=-TWO_PI,
            op0=ALU.is_gt, op1=ALU.mult,
        )
        nc.vector.tensor_add(out=phase[:], in0=phase[:], in1=wrap[:])
        sin_cos = const.tile([P, 2, TOK_TILES, HALF_ROPE], F32, name="sin_cos")
        nc.scalar.activation(
            out=sin_cos[:].rearrange("p s i j -> p s (i j)"), in_=phase[:], func=ACT.Sin
        )
        nc.scalar.activation(out=table_warmer[:], in_=table_warmer[:], func=ACT.Sqrt)

        ks_stage = [
            [
                keep.tile(
                    [P, GROUP, BATCH_TILES[batch], NOPE + ROPE], F32,
                    name="ks_stage%d%d" % (batch, b),
                )
                for b in range(2)
            ]
            for batch in range(2)
        ]
        both = [P, TOK_TILES, 2, HALF_ROPE]
        by_sin = const.tile(both, F32, name="by_sin")
        by_cos = const.tile(both, F32, name="by_cos")
        rotated = const.tile(both, F32, name="rotated")

        def rotate_k_pe():
            nc.vector.tensor_tensor(
                out=by_sin[:], in0=kp[:], in1=sin_cos[:, 0].unsqueeze(2).to_broadcast(both),
                op=ALU.mult,
            )
            nc.vector.tensor_tensor(
                out=by_cos[:], in0=kp[:], in1=sin_cos[:, 1].unsqueeze(2).to_broadcast(both),
                op=ALU.mult,
            )
            nc.vector.tensor_tensor(
                out=rotated[:, :, 0, :], in0=by_cos[:, :, 0, :], in1=by_sin[:, :, 1, :],
                op=ALU.subtract,
            )
            nc.vector.tensor_tensor(
                out=rotated[:, :, 1, :], in0=by_sin[:, :, 0, :], in1=by_cos[:, :, 1, :],
                op=ALU.add,
            )

        def fill_rope(batch):
            for stage in ks_stage[batch]:
                nc.vector.tensor_copy(
                    out=stage[:, :, :, NOPE:],
                    in_=rotated[:, batch_slice(batch), :, :]
                    .rearrange("p i s j -> p i (s j)")
                    .unsqueeze(1)
                    .to_broadcast([P, GROUP, BATCH_TILES[batch], ROPE]),
                )

        gain = const.tile([P, PACK, P], F32, name="gain")

        gain_ps = psum.tile([P, KVR], F32, tag="bank", name="gain_ps")
        nc.tensor.matmul(gain_ps[:], lhsT=ones[:], rhs=gain_row[:], start=True, stop=True)

        def keep_gain():
            nc.vector.tensor_copy(
                out=gain[:], in_=gain_ps[:].rearrange("p (q t) -> p t q", t=PACK)
            )

        def codes_and_scales(name, width):
            codes = keep.tile([P, width], U32, name=name + "_codes", align_bytes=64)
            scales = keep.tile([P, width], U8, name=name + "_scales", align_bytes=64)
            return codes, scales

        x_q = [codes_and_scales("x%d" % i, X_PASSES * P) for i in range(TOK_TILES)]
        wc_q = [codes_and_scales("wc%d" % g, KVR) for g in range(X_PASSES)]
        cn_q = [codes_and_scales("cn%d" % i, P) for i in range(TOK_TILES)]
        wv_q = [codes_and_scales("wv%d" % m, GROUP * VD) for m in range(GROUPS)]
        wk_q = [codes_and_scales("wk%d" % m, GROUP * NOPE) for m in range(GROUPS)]

        def quantise(grouped, pair):
            codes, scales = pair
            nc.vector.quantize_mx(
                out=codes[:].bitcast(FP8X4), scales=scales[:], in_=grouped
            )

        def mx(out, lhs, lhs_cols, rhs, start, stop):
            nc.tensor.matmul_mx(
                out=out,
                lhsT=lhs[0][:, lhs_cols].bitcast(FP8X4),
                lhsT_scale=lhs[1][:, lhs_cols],
                rhs=rhs[0][:].bitcast(FP8X4),
                rhs_scale=rhs[1][:],
                start=start,
                stop=stop,
            )

        def leave_psum(which, out, in_):
            if which % 2 == 0:
                nc.scalar.copy(out=out, in_=in_)
            else:
                nc.vector.tensor_copy(out=out, in_=in_)

        x_grouped = {}
        cn_rows = {}

        def transpose_x(i):
            words = x_rows[i][:].bitcast(F32)
            grouped = work.tile(
                [P, X_PASSES * P * PACK], BF16, tag="grouped", bufs=4, align_bytes=64,
                name="x_grouped",
            )
            grouped_words = grouped[:].bitcast(F32)
            for bank in range(2):
                xt = psum.tile([P, 4, P], F32, tag="bank", name="xt")
                for s in range(4):
                    chunk = 4 * bank + s
                    nc.tensor.transpose(
                        xt[:, s, :], words[:, P * chunk : P * (chunk + 1)], ident_f32[:]
                    )
                leave_psum(
                    0,
                    grouped_words[:, 512 * bank : 512 * (bank + 1)].rearrange(
                        "p (g r u) -> p g r u", g=2, u=2
                    ),
                    xt[:].rearrange("p (g u) r -> p g r u", u=2),
                )
            x_grouped[i] = grouped

        def quantise_x(i):
            quantise(x_grouped[i][:], x_q[i])

        def project(i):
            acc = psum.tile([P, KVR], F32, tag="bank", name="acc")
            for g in range(X_PASSES):
                mx(acc[:], x_q[i], slice(P * g, P * (g + 1)), wc_q[g],
                   g == 0, g == X_PASSES - 1)
            squares = work.tile([P, KVR], BF16, tag="squares", name="squares")
            mean_sq = work.tile([P, 1], F32, tag="mean_sq", name="mean_sq")
            nc.scalar.activation(
                out=squares[:], in_=acc[:], func=ACT.Square,
                scale=1.0 / math.sqrt(KVR), accum_out=mean_sq[:],
            )
            rms = work.tile([P, 1], F32, tag="rms", name="rms")
            nc.scalar.activation(out=rms[:], in_=mean_sq[:], func=ACT.Sqrt, bias=EPS)
            inv_rms = work.tile([P, 1], F32, tag="inv_rms", name="inv_rms")
            nc.vector.reciprocal(out=inv_rms[:], in_=rms[:])
            cn = work.tile([P, PACK, P], BF16, tag="cn", bufs=max(BATCH_TILES), name="cn")
            nc.vector.scalar_tensor_tensor(
                out=cn[:],
                in0=acc[:].rearrange("p (q t) -> p t q", t=PACK),
                scalar=inv_rms[:, 0:1],
                in1=gain[:],
                op0=ALU.mult,
                op1=ALU.mult,
            )
            cn_rows[i] = cn

        def transpose_cn(i):
            cn_t = psum.tile([P, PACK, P], BF16, tag="bank", name="cn_t")
            for t in range(PACK):
                nc.tensor.transpose(cn_t[:, t, :], cn_rows[i][:, t, :], ident_bf16[:])
            grouped = work.tile(
                [P, P, PACK], BF16, tag="cn_grouped", align_bytes=64, name="cn_grouped"
            )
            nc.scalar.copy(out=grouped[:], in_=cn_t[:].rearrange("p t r -> p r t"))
            quantise(grouped[:].rearrange("p r t -> p (r t)"), cn_q[i])

        def grouped_columns(width):
            grouped = work.tile(
                [P, X_PASSES * P * PACK], BF16, tag="grouped", bufs=4, align_bytes=64,
                name="w_grouped",
            )
            return grouped[:, 0 : width * PACK]

        def regroup_wc(g):
            flat = grouped_columns(KVR)
            dst = flat.rearrange("p (c i t) -> p c t i", i=RUN, t=PACK)
            src = wc_raw[g][:].rearrange("p t (c i) -> p c t i", i=RUN)
            middle = KVR // RUN // 2
            nc.scalar.copy(out=dst[:, 0:middle], in_=src[:, 0:middle])
            nc.vector.tensor_copy(out=dst[:, middle:], in_=src[:, middle:])
            return flat

        def regroup_wb(m, first, width):
            flat = grouped_columns(GROUP * width)
            heads = wb_raw[m][:].rearrange("p t (h f) -> p t h f", f=HEAD_COLS)
            nc.vector.tensor_copy(
                out=flat.rearrange("p (h c i t) -> p h c t i", h=GROUP, i=RUN, t=PACK),
                in_=heads[:, :, :, first : first + width].rearrange(
                    "p t h (c i) -> p h c t i", i=RUN
                ),
            )
            return flat

        def vector_takes(batch, n):
            if batch == 0:
                return 1 if n % 4 == 3 else 0
            return n % 2

        def v_unit(m, batch):
            tiles = BATCH_TILES[batch]
            stage = work.tile([P, GROUP, tiles, VD], F32, tag="v_stage", bufs=3, name="v_stage")
            for s in range(tiles):
                kv = psum.tile([P, GROUP * VD], F32, tag="bank", name="kv")
                mx(kv[:], cn_q[BATCH_START[batch] + s], slice(0, P), wv_q[m], True, True)
                leave_psum(
                    vector_takes(batch, s),
                    stage[:, :, s, :],
                    kv[:].rearrange("p (h d) -> p h d", h=GROUP),
                )
            nc.sync.dma_start(
                out=v_view[:, GROUP * m : GROUP * (m + 1), batch_slice(batch), :], in_=stage[:]
            )

        def k_unit(m, batch):
            tiles = BATCH_TILES[batch]
            stage = ks_stage[batch][m % 2]
            for first in range(0, tiles, 2):
                count = min(2, tiles - first)
                kk = psum.tile([P, 2, GROUP * NOPE], F32, tag="bank", name="kk")
                for s in range(count):
                    mx(kk[:, s, :], cn_q[BATCH_START[batch] + first + s], slice(0, P),
                       wk_q[m], True, True)
                leave_psum(
                    vector_takes(batch, 2 + first // 2),
                    stage[:, :, first : first + count, 0:NOPE].rearrange("p h i d -> p i h d"),
                    kk[:, 0:count, :].rearrange("p i (h d) -> p i h d", h=GROUP),
                )
            nc.sync.dma_start(
                out=ks_view[:, GROUP * m : GROUP * (m + 1), batch_slice(batch), :], in_=stage[:]
            )

        def unit(u, batch):
            if u % 2 == 0:
                v_unit(u // 2, batch)
            else:
                k_unit(u // 2, batch)

        unit_flats = {}

        def regroup_unit(u):
            if u % 2 == 0:
                unit_flats[u] = regroup_wb(u // 2, NOPE, VD)
            else:
                unit_flats[u] = regroup_wb(u // 2, 0, NOPE)

        def quantise_unit(u):
            quantise(unit_flats[u], wv_q[u // 2] if u % 2 == 0 else wk_q[u // 2])

        flats = {}
        for g in range(X_PASSES):
            flats[g] = regroup_wc(g)
            if g > 0:
                quantise(flats[g - 1], wc_q[g - 1])
        rotate_k_pe()
        quantise(flats[X_PASSES - 1], wc_q[X_PASSES - 1])

        for i in batch_tiles(0):
            transpose_x(i)
            if i == 1:
                keep_gain()
            if i > 0:
                quantise_x(i - 1)
        quantise_x(BATCH_TILES[0] - 1)
        for i in batch_tiles(0):
            project(i)
            if i == 0:
                regroup_unit(0)
        quantise_unit(0)
        for i in batch_tiles(0):
            transpose_cn(i)
        regroup_unit(1)

        second = BATCH_START[1]
        tiles = BATCH_TILES[1]
        for u in range(UNITS):
            if u + 1 < UNITS:
                quantise_unit(u + 1)
            unit(u, 0)
            if u == 0:
                fill_rope(0)
            if u + 2 < UNITS:
                regroup_unit(u + 2)
            if u < tiles:
                transpose_x(second + u)
            if 1 <= u < tiles + 1:
                quantise_x(second + u - 1)
            if 2 <= u < tiles + 2:
                project(second + u - 2)
            if 4 <= u < tiles + 4:
                transpose_cn(second + u - 4)

        fill_rope(1)
        for u in range(UNITS):
            unit(u, 1)
